import numpy as np
import ml_dtypes


def mxq(x, axis, fmt="e4m3"):
    dtype, down = {"e4m3": (ml_dtypes.float8_e4m3fn, 7), "e5m2": (ml_dtypes.float8_e5m2, 14)}[fmt]
    v = np.moveaxis(np.asarray(x, np.float32).astype(ml_dtypes.bfloat16).astype(np.float64), axis, -1)
    blocks = v.reshape(v.shape[:-1] + (-1, 32))
    amax = np.abs(blocks).max(-1, keepdims=True)
    byte = np.maximum(np.where(amax > 0, np.frexp(amax)[1] - 1 + 127, 0) - down, 1)
    scale = np.exp2(byte - 127.0)
    codes = (blocks / scale).astype(np.float32).astype(dtype).astype(np.float64)
    return np.moveaxis((codes * scale).reshape(v.shape), -1, axis)


WIDE = False


def mx_kscale(k):
    if not WIDE:
        return np.ones(k)
    levels = np.array([10, -10, 5, -5, 0])
    a = np.random.permutation(np.resize(levels, k // 512 * 4)).reshape(k // 512, 4)
    idx = np.arange(k)
    return np.exp2(a[idx // 512, idx % 128 // 32])


BF16 = ml_dtypes.bfloat16


def bf(x):
    return np.asarray(x, np.float32).astype(BF16)


def f64(x):
    return np.asarray(x).astype(np.float64)


B, CI, CO, OH, OW, K = 64, 64, 64, 4, 4, 4
STRIDE = 1
IH, IW = (OH - 1) * STRIDE + K, (OW - 1) * STRIDE + K
P = OH * OW
KC = CI * K * K


def extract_patches(x, out_h, out_w, k, stride):
    rows = []
    for di in range(k):
        cols = []
        for dj in range(k):
            cols.append(x[:, :, di:di + out_h * stride:stride, dj:dj + out_w * stride:stride])
        rows.append(np.stack(cols, axis=2))
    return np.stack(rows, axis=2)


def setup_inputs():
    s = mx_kscale(KC).reshape(CI, K * K)[:, 0]
    return {"in_spikes": bf(np.random.uniform(0.0, 1.0, (B, CI, IH, IW)) * s[None, :, None, None]),
            "weights": bf(np.random.standard_normal((OH, OW, CI, K, K, CO)) * 1.5 / np.sqrt(KC) / s[None, None, :, None, None, None])}


def reference(in_spikes, weights):
    out_h, out_w, _, k, _, _ = weights.shape
    patches = extract_patches(f64(in_spikes), out_h, out_w, k, STRIDE)
    p = patches.reshape(B, KC, P).transpose(2, 0, 1)
    w = f64(weights).reshape(P, KC, CO)
    out = mxq(p, 2, "e4m3") @ mxq(w, 1, "e4m3")
    return out.transpose(1, 2, 0).reshape(B, CO, OH, OW)

@@ -1,0 +1,115 @@
+import concourse.mybir as mybir
+from concourse.masks import make_identity
+
+BF16 = mybir.dt.bfloat16
+F32 = mybir.dt.float32
+I32 = mybir.dt.int32
+U32 = mybir.dt.uint32
+U8 = mybir.dt.uint8
+FP8X4 = mybir.dt.float8_e4m3fn_x4
+
+P = 128
+B = 64
+CI = 64
+CO = 64
+IH = 7
+OH = 4
+KW = 4
+PASSES = 2
+CL = CI // PASSES
+SLOT = 64
+ROW_SLOTS = PASSES * OH
+FLOPS = 2 * OH * OH * B * CI * KW * KW * CO
+
+
+def tile_stdpconvinhibit_s_kernel(tc, in_spikes, weights, out):
+    nc = tc.nc
+    with tc.tile_pool(name="keep", bufs=1) as keep, tc.psum_pool(name="psum", bufs=1) as psum:
+        x_sb = keep.tile([P, CL * IH * IH], BF16, name="x_sb")
+        nc.sync.dma_start(out=x_sb[:], in_=in_spikes.rearrange("b (h c) r s -> (b h) (c r s)", h=PASSES))
+        w_raw = []
+        for i in range(OH):
+            raw = keep.tile([P, ROW_SLOTS, KW, CO], BF16, name="w_raw%d" % i)
+            nc.sync.dma_start(
+                out=raw[:].rearrange("p g v k -> p g (v k)"),
+                in_=weights[i].rearrange("j (h c) u v k -> (c u) (j h) (v k)", h=PASSES),
+            )
+            w_raw.append(raw)
+
+        ident = keep.tile([P, P], BF16, name="ident")
+        make_identity(nc, ident[:])
+
+        n_slots = 1 + OH * ROW_SLOTS
+        p_codes = keep.tile([P, n_slots * SLOT], U32, name="p_codes", align_bytes=64)
+        p_scales = keep.tile([P, n_slots * SLOT], U8, name="p_scales", align_bytes=64)
+        w_codes = keep.tile([P, n_slots * SLOT], U32, name="w_codes", align_bytes=64)
+        w_scales = keep.tile([P, n_slots * SLOT], U8, name="w_scales", align_bytes=64)
+        for codes in (p_codes, w_codes):
+            nc.vector.memset(codes[:, 0:SLOT].bitcast(I32), 0)
+        for scales in (p_scales, w_scales):
+            nc.vector.memset(scales[:, 0:SLOT].bitcast(I32), 0)
+
+        x_img = x_sb[:].rearrange("p (c r s) -> p c r s", c=CL, r=IH, s=IH)
+        x_cols = keep.tile([P, OH, IH, CL, KW], BF16, name="x_cols")
+        for i in range(OH):
+            src = x_img[:, :, i : i + KW, :].rearrange("p c u s -> p s c u")
+            if i == OH - 1:
+                nc.scalar.copy(out=x_cols[:, i], in_=src)
+            else:
+                nc.vector.tensor_copy(out=x_cols[:, i], in_=src)
+
+        x_t = []
+        for i in range(OH):
+            bank = psum.tile([P, IH, P], BF16, name="x_t%d" % i)
+            for s in range(IH):
+                nc.tensor.transpose(bank[:, s, :], x_cols[:, i, s].rearrange("p c u -> p (c u)"), ident[:])
+            x_t.append(bank)
+
+        result = keep.tile([P, CO, OH * OH], F32, name="result")
+        for i in range(OH):
+            row = slice((1 + i * ROW_SLOTS) * SLOT, (1 + (i + 1) * ROW_SLOTS) * SLOT)
+            w_grouped = keep.tile([P, ROW_SLOTS, CO, KW], BF16, name="w_grouped%d" % i, align_bytes=64)
+            nc.vector.tensor_copy(
+                out=w_grouped[:].rearrange("p g (c e) v -> p g c v e", e=4),
+                in_=w_raw[i][:].rearrange("p g v (c e) -> p g c v e", e=4),
+            )
+            p_grouped = keep.tile([P, PASSES, OH, B, KW], BF16, name="p_grouped%d" % i, align_bytes=64)
+            for j in range(OH):
+                nc.scalar.copy(
+                    out=p_grouped[:, :, j],
+                    in_=x_t[i][:, j : j + KW, :].rearrange("p v (b h) -> p h b v", h=PASSES),
+                )
+            nc.vector.quantize_mx(
+                out=w_codes[:, row].bitcast(FP8X4),
+                scales=w_scales[:, row],
+                in_=w_grouped[:].rearrange("p g k v -> p (g k v)"),
+            )
+            nc.vector.quantize_mx(
+                out=p_codes[:, row].bitcast(FP8X4),
+                scales=p_scales[:, row],
+                in_=p_grouped[:].rearrange("p h j b v -> p (h j b v)"),
+            )
+            acc = psum.tile([P, OH, 2 * SLOT], F32, name="acc%d" % i)
+            for j in range(OH):
+                for h in range(PASSES):
+                    p_slot = 1 + i * ROW_SLOTS + h * OH + j
+                    w_slot = 1 + i * ROW_SLOTS + j * PASSES + h
+                    p_win = slice((p_slot - 1) * SLOT, (p_slot + 1) * SLOT)
+                    w_win = slice((w_slot - 1) * SLOT, (w_slot + 1) * SLOT)
+                    nc.tensor.matmul_mx(
+                        out=acc[:, j, :],
+                        lhsT=p_codes[:, p_win].bitcast(FP8X4),
+                        lhsT_scale=p_scales[:, p_win],
+                        rhs=w_codes[:, w_win].bitcast(FP8X4),
+                        rhs_scale=w_scales[:, w_win],
+                        start=(h == 0),
+                        stop=(h == PASSES - 1),
+                    )
+            nc.vector.tensor_copy(
+                out=result[B:P, :, i * OH : (i + 1) * OH],
+                in_=acc[B:P, :, SLOT : 2 * SLOT].rearrange("p j k -> p k j"),
+            )
+        nc.sync.dma_start(
+            out=out.rearrange("b k i j -> b (k i j)"),
+            in_=result[B:P].rearrange("p k q -> p (k q)"),
+        )

@@ -18,28 +18,31 @@ KW = 4
 PASSES = 2
 CL = CI // PASSES
 SLOT = 64
-ROW_SLOTS = PASSES * OH
+PAIR = 2
+UNITS = OH * OH // PAIR
+UNIT_SLOTS = PAIR * PASSES
 FLOPS = 2 * OH * OH * B * CI * KW * KW * CO
 
 
 def tile_stdpconvinhibit_s_kernel(tc, in_spikes, weights, out):
     nc = tc.nc
-    with tc.tile_pool(name="keep", bufs=1) as keep, tc.psum_pool(name="psum", bufs=1) as psum:
+    with tc.tile_pool(name="keep", bufs=1) as keep, tc.psum_pool(name="psum", bufs=1) as psum, tc.manual_schedule():
         x_sb = keep.tile([P, CL * IH * IH], BF16, name="x_sb")
         nc.sync.dma_start(out=x_sb[:], in_=in_spikes.rearrange("b (h c) r s -> (b h) (c r s)", h=PASSES))
         w_raw = []
-        for i in range(OH):
-            raw = keep.tile([P, ROW_SLOTS, KW, CO], BF16, name="w_raw%d" % i)
+        for u in range(UNITS):
+            i, j0 = divmod(u * PAIR, OH)
+            raw = keep.tile([P, UNIT_SLOTS, KW, CO], BF16, name="w_raw%d" % u)
             nc.sync.dma_start(
                 out=raw[:].rearrange("p g v k -> p g (v k)"),
-                in_=weights[i].rearrange("j (h c) u v k -> (c u) (j h) (v k)", h=PASSES),
+                in_=weights[i, j0 : j0 + PAIR].rearrange("j (h c) u v k -> (c u) (j h) (v k)", h=PASSES),
             )
             w_raw.append(raw)
 
         ident = keep.tile([P, P], BF16, name="ident")
         make_identity(nc, ident[:])
 
-        n_slots = 1 + OH * ROW_SLOTS
+        n_slots = 1 + UNITS * UNIT_SLOTS
         p_codes = keep.tile([P, n_slots * SLOT], U32, name="p_codes", align_bytes=64)
         p_scales = keep.tile([P, n_slots * SLOT], U8, name="p_scales", align_bytes=64)
         w_codes = keep.tile([P, n_slots * SLOT], U32, name="w_codes", align_bytes=64)
@@ -65,39 +68,55 @@ def tile_stdpconvinhibit_s_kernel(tc, in_spikes, weights, out):
                 nc.tensor.transpose(bank[:, s, :], x_cols[:, i, s].rearrange("p c u -> p (c u)"), ident[:])
             x_t.append(bank)
 
-        result = keep.tile([P, CO, OH * OH], F32, name="result")
-        for i in range(OH):
-            row = slice((1 + i * ROW_SLOTS) * SLOT, (1 + (i + 1) * ROW_SLOTS) * SLOT)
-            w_grouped = keep.tile([P, ROW_SLOTS, CO, KW], BF16, name="w_grouped%d" % i, align_bytes=64)
+        acc = [psum.tile([P, OH, 2 * SLOT], F32, name="acc%d" % i) for i in range(OH)]
+        w_grouped = [
+            keep.tile([P, UNIT_SLOTS, CO, KW], BF16, name="w_grouped%d" % u, align_bytes=64) for u in range(UNITS)
+        ]
+        p_grouped = [
+            keep.tile([P, PASSES, PAIR, B, KW], BF16, name="p_grouped%d" % u, align_bytes=64) for u in range(UNITS)
+        ]
+
+        def unit_columns(u):
+            return slice((1 + u * UNIT_SLOTS) * SLOT, (1 + (u + 1) * UNIT_SLOTS) * SLOT)
+
+        def regroup_weights(u):
             nc.vector.tensor_copy(
-                out=w_grouped[:].rearrange("p g (c e) v -> p g c v e", e=4),
-                in_=w_raw[i][:].rearrange("p g v (c e) -> p g c v e", e=4),
+                out=w_grouped[u][:].rearrange("p g (c e) v -> p g c v e", e=4),
+                in_=w_raw[u][:].rearrange("p g v (c e) -> p g c v e", e=4),
             )
-            p_grouped = keep.tile([P, PASSES, OH, B, KW], BF16, name="p_grouped%d" % i, align_bytes=64)
-            for j in range(OH):
+
+        def quantise_weights(u):
+            nc.vector.quantize_mx(
+                out=w_codes[:, unit_columns(u)].bitcast(FP8X4),
+                scales=w_scales[:, unit_columns(u)],
+                in_=w_grouped[u][:].rearrange("p g k v -> p (g k v)"),
+            )
+
+        def copy_patches(u):
+            i, j0 = divmod(u * PAIR, OH)
+            for e in range(PAIR):
                 nc.scalar.copy(
-                    out=p_grouped[:, :, j],
-                    in_=x_t[i][:, j : j + KW, :].rearrange("p v (b h) -> p h b v", h=PASSES),
+                    out=p_grouped[u][:, :, e],
+                    in_=x_t[i][:, j0 + e : j0 + e + KW, :].rearrange("p v (b h) -> p h b v", h=PASSES),
                 )
+
+        def quantise_patches(u):
             nc.vector.quantize_mx(
-                out=w_codes[:, row].bitcast(FP8X4),
-                scales=w_scales[:, row],
-                in_=w_grouped[:].rearrange("p g k v -> p (g k v)"),
+                out=p_codes[:, unit_columns(u)].bitcast(FP8X4),
+                scales=p_scales[:, unit_columns(u)],
+                in_=p_grouped[u][:].rearrange("p h e b v -> p (h e b v)"),
             )
-            nc.vector.quantize_mx(
-                out=p_codes[:, row].bitcast(FP8X4),
-                scales=p_scales[:, row],
-                in_=p_grouped[:].rearrange("p h j b v -> p (h j b v)"),
-            )
-            acc = psum.tile([P, OH, 2 * SLOT], F32, name="acc%d" % i)
-            for j in range(OH):
+
+        def multiply(u):
+            i, j0 = divmod(u * PAIR, OH)
+            for e in range(PAIR):
                 for h in range(PASSES):
-                    p_slot = 1 + i * ROW_SLOTS + h * OH + j
-                    w_slot = 1 + i * ROW_SLOTS + j * PASSES + h
+                    p_slot = 1 + u * UNIT_SLOTS + h * PAIR + e
+                    w_slot = 1 + u * UNIT_SLOTS + e * PASSES + h
                     p_win = slice((p_slot - 1) * SLOT, (p_slot + 1) * SLOT)
                     w_win = slice((w_slot - 1) * SLOT, (w_slot + 1) * SLOT)
                     nc.tensor.matmul_mx(
-                        out=acc[:, j, :],
+                        out=acc[i][:, j0 + e, :],
                         lhsT=p_codes[:, p_win].bitcast(FP8X4),
                         lhsT_scale=p_scales[:, p_win],
                         rhs=w_codes[:, w_win].bitcast(FP8X4),
@@ -105,9 +124,23 @@ def tile_stdpconvinhibit_s_kernel(tc, in_spikes, weights, out):
                         start=(h == 0),
                         stop=(h == PASSES - 1),
                     )
-            nc.vector.tensor_copy(
+
+        for u in range(UNITS):
+            copy_patches(u)
+            regroup_weights(u)
+            if u > 0:
+                quantise_patches(u - 1)
+            quantise_weights(u)
+            if u > 0:
+                multiply(u - 1)
+        quantise_patches(UNITS - 1)
+        multiply(UNITS - 1)
+
+        result = keep.tile([P, CO, OH * OH], F32, name="result")
+        for i in range(OH):
+            nc.scalar.copy(
                 out=result[B:P, :, i * OH : (i + 1) * OH],
-                in_=acc[B:P, :, SLOT : 2 * SLOT].rearrange("p j k -> p k j"),
+                in_=acc[i][B:P, :, SLOT : 2 * SLOT].rearrange("p j k -> p k j"),
             )
         nc.sync.dma_start(
             out=out.rearrange("b k i j -> b (k i j)"),

@@ -55,11 +55,14 @@ def tile_stdpconvinhibit_s_kernel(tc, in_spikes, weights, out):
         x_img = x_sb[:].rearrange("p (c r s) -> p c r s", c=CL, r=IH, s=IH)
         x_cols = keep.tile([P, OH, IH, CL, KW], BF16, name="x_cols")
         for i in range(OH):
-            src = x_img[:, :, i : i + KW, :].rearrange("p c u s -> p s c u")
-            if i == OH - 1:
-                nc.scalar.copy(out=x_cols[:, i], in_=src)
-            else:
-                nc.vector.tensor_copy(out=x_cols[:, i], in_=src)
+            for s0 in range(0, IH, KW):
+                s1 = min(s0 + KW, IH)
+                src = x_img[:, :, i : i + KW, s0:s1]
+                dst = x_cols[:, i, s0:s1].rearrange("p s c u -> p c u s")
+                if i == OH - 1:
+                    nc.scalar.copy(out=dst, in_=src)
+                else:
+                    nc.vector.tensor_copy(out=dst, in_=src)
 
         x_t = []
         for i in range(OH):

@@ -21,12 +21,17 @@ SLOT = 64
 PAIR = 2
 UNITS = OH * OH // PAIR
 UNIT_SLOTS = PAIR * PASSES
+RUN = 6
+WORDS = RUN // 2
+SCALAR_REGROUPS = (5, 6, 7)
 FLOPS = 2 * OH * OH * B * CI * KW * KW * CO
 
 
 def tile_stdpconvinhibit_s_kernel(tc, in_spikes, weights, out):
     nc = tc.nc
-    with tc.tile_pool(name="keep", bufs=1) as keep, tc.psum_pool(name="psum", bufs=1) as psum, tc.manual_schedule():
+    with tc.tile_pool(name="keep", bufs=1) as keep, tc.psum_pool(name="psum", bufs=1) as psum, tc.psum_pool(
+        name="turned", bufs=4
+    ) as turned, tc.manual_schedule():
         x_sb = keep.tile([P, CL * IH * IH], BF16, name="x_sb")
         nc.sync.dma_start(out=x_sb[:], in_=in_spikes.rearrange("b (h c) r s -> (b h) (c r s)", h=PASSES))
         w_raw = []
@@ -39,7 +44,7 @@ def tile_stdpconvinhibit_s_kernel(tc, in_spikes, weights, out):
             )
             w_raw.append(raw)
 
-        ident = keep.tile([P, P], BF16, name="ident")
+        ident = keep.tile([P, P], F32, name="ident")
         make_identity(nc, ident[:])
 
         n_slots = 1 + UNITS * UNIT_SLOTS
@@ -53,23 +58,25 @@ def tile_stdpconvinhibit_s_kernel(tc, in_spikes, weights, out):
             nc.vector.memset(scales[:, 0:SLOT].bitcast(I32), 0)
 
         x_img = x_sb[:].rearrange("p (c r s) -> p c r s", c=CL, r=IH, s=IH)
-        x_cols = keep.tile([P, OH, IH, CL, KW], BF16, name="x_cols")
-        for i in range(OH):
-            for s0 in range(0, IH, KW):
-                s1 = min(s0 + KW, IH)
-                src = x_img[:, :, i : i + KW, s0:s1]
-                dst = x_cols[:, i, s0:s1].rearrange("p s c u -> p c u s")
-                if i == OH - 1:
-                    nc.scalar.copy(out=dst, in_=src)
-                else:
-                    nc.vector.tensor_copy(out=dst, in_=src)
+        x_runs = [keep.tile([P, 2, CL, KW, RUN], BF16, name="x_runs%d" % i) for i in range(OH)]
+        x_t = {}
 
-        x_t = []
-        for i in range(OH):
-            bank = psum.tile([P, IH, P], BF16, name="x_t%d" % i)
-            for s in range(IH):
-                nc.tensor.transpose(bank[:, s, :], x_cols[:, i, s].rearrange("p c u -> p (c u)"), ident[:])
-            x_t.append(bank)
+        def lay_out_rows(i):
+            for parity in range(2):
+                nc.vector.tensor_copy(out=x_runs[i][:, parity], in_=x_img[:, :, i : i + KW, parity : parity + RUN])
+
+        def transpose_rows(i):
+            for parity in range(2):
+                words = (
+                    x_runs[i][:, parity]
+                    .rearrange("p c u s -> p (c u s)")
+                    .bitcast(F32)
+                    .rearrange("p (n w) -> p n w", w=WORDS)
+                )
+                bank = turned.tile([P, WORDS, P], F32, name="x_t")
+                for w in range(WORDS):
+                    nc.tensor.transpose(bank[:, w, :], words[:, :, w], ident[:])
+                x_t[(i, parity)] = bank
 
         acc = [psum.tile([P, OH, 2 * SLOT], F32, name="acc%d" % i) for i in range(OH)]
         w_grouped = [
@@ -83,10 +90,12 @@ def tile_stdpconvinhibit_s_kernel(tc, in_spikes, weights, out):
             return slice((1 + u * UNIT_SLOTS) * SLOT, (1 + (u + 1) * UNIT_SLOTS) * SLOT)
 
         def regroup_weights(u):
-            nc.vector.tensor_copy(
-                out=w_grouped[u][:].rearrange("p g (c e) v -> p g c v e", e=4),
-                in_=w_raw[u][:].rearrange("p g v (c e) -> p g c v e", e=4),
-            )
+            dst = w_grouped[u][:].rearrange("p g (c e) v -> p g c v e", e=4)
+            src = w_raw[u][:].rearrange("p g v (c e) -> p g c v e", e=4)
+            if u in SCALAR_REGROUPS:
+                nc.scalar.copy(out=dst, in_=src)
+            else:
+                nc.vector.tensor_copy(out=dst, in_=src)
 
         def quantise_weights(u):
             nc.vector.quantize_mx(
@@ -98,9 +107,10 @@ def tile_stdpconvinhibit_s_kernel(tc, in_spikes, weights, out):
         def copy_patches(u):
             i, j0 = divmod(u * PAIR, OH)
             for e in range(PAIR):
+                j = j0 + e
                 nc.scalar.copy(
-                    out=p_grouped[u][:, :, e],
-                    in_=x_t[i][:, j0 + e : j0 + e + KW, :].rearrange("p v (b h) -> p h b v", h=PASSES),
+                    out=p_grouped[u][:, :, e].bitcast(F32),
+                    in_=x_t[(i, j % 2)][:, j // 2 : j // 2 + 2, :].rearrange("p w (b h) -> p h b w", h=PASSES),
                 )
 
         def quantise_patches(u):
@@ -128,23 +138,38 @@ def tile_stdpconvinhibit_s_kernel(tc, in_spikes, weights, out):
                         stop=(h == PASSES - 1),
                     )
 
+        result = keep.tile([P, CO, OH * OH], F32, name="result")
+
+        def copy_result(i):
+            nc.scalar.copy(
+                out=result[B:P, :, i * OH : (i + 1) * OH],
+                in_=acc[i][B:P, :, SLOT : 2 * SLOT].rearrange("p j k -> p k j"),
+            )
+
+        lay_out_rows(0)
+        transpose_rows(0)
+        lay_out_rows(1)
+        transpose_rows(1)
         for u in range(UNITS):
             copy_patches(u)
-            regroup_weights(u)
+            if u % PAIR == 1 and u // PAIR + 2 < OH:
+                lay_out_rows(u // PAIR + 2)
+                transpose_rows(u // PAIR + 2)
+            if u >= 3 and u + 2 in SCALAR_REGROUPS:
+                regroup_weights(u + 2)
+            if u not in SCALAR_REGROUPS:
+                regroup_weights(u)
             if u > 0:
                 quantise_patches(u - 1)
             quantise_weights(u)
             if u > 0:
                 multiply(u - 1)
+            if u >= 3 and u % PAIR == 1:
+                copy_result(u // PAIR - 1)
         quantise_patches(UNITS - 1)
         multiply(UNITS - 1)
+        copy_result(OH - 1)
 
-        result = keep.tile([P, CO, OH * OH], F32, name="result")
-        for i in range(OH):
-            nc.scalar.copy(
-                out=result[B:P, :, i * OH : (i + 1) * OH],
-                in_=acc[i][B:P, :, SLOT : 2 * SLOT].rearrange("p j k -> p k j"),
-            )
         nc.sync.dma_start(
             out=out.rearrange("b k i j -> b (k i j)"),
             in_=result[B:P].rearrange("p k q -> p (k q)"),

@@ -23,7 +23,7 @@ UNITS = OH * OH // PAIR
 UNIT_SLOTS = PAIR * PASSES
 RUN = 6
 WORDS = RUN // 2
-SCALAR_REGROUPS = (5, 6, 7)
+SCALAR_REGROUPS = ()
 FLOPS = 2 * OH * OH * B * CI * KW * KW * CO
 
 

@@ -63,7 +63,11 @@ def tile_stdpconvinhibit_s_kernel(tc, in_spikes, weights, out):
 
         def lay_out_rows(i):
             for parity in range(2):
-                nc.vector.tensor_copy(out=x_runs[i][:, parity], in_=x_img[:, :, i : i + KW, parity : parity + RUN])
+                src = x_img[:, :, i : i + KW, parity : parity + RUN]
+                if i == 0:
+                    nc.vector.tensor_copy(out=x_runs[i][:, parity], in_=src)
+                else:
+                    nc.scalar.copy(out=x_runs[i][:, parity], in_=src)
 
         def transpose_rows(i):
             for parity in range(2):
@@ -147,8 +151,8 @@ def tile_stdpconvinhibit_s_kernel(tc, in_spikes, weights, out):
             )
 
         lay_out_rows(0)
-        transpose_rows(0)
         lay_out_rows(1)
+        transpose_rows(0)
         transpose_rows(1)
         for u in range(UNITS):
             copy_patches(u)

@@ -33,9 +33,10 @@ def tile_stdpconvinhibit_s_kernel(tc, in_spikes, weights, out):
         name="turned", bufs=4
     ) as turned, tc.manual_schedule():
         x_sb = keep.tile([P, CL * IH * IH], BF16, name="x_sb")
-        nc.sync.dma_start(out=x_sb[:], in_=in_spikes.rearrange("b (h c) r s -> (b h) (c r s)", h=PASSES))
         w_raw = []
         for u in range(UNITS):
+            if u == 1:
+                nc.sync.dma_start(out=x_sb[:], in_=in_spikes.rearrange("b (h c) r s -> (b h) (c r s)", h=PASSES))
             i, j0 = divmod(u * PAIR, OH)
             raw = keep.tile([P, UNIT_SLOTS, KW, CO], BF16, name="w_raw%d" % u)
             nc.sync.dma_start(
@@ -150,28 +151,26 @@ def tile_stdpconvinhibit_s_kernel(tc, in_spikes, weights, out):
                 in_=acc[i][B:P, :, SLOT : 2 * SLOT].rearrange("p j k -> p k j"),
             )
 
+        regroup_weights(0)
         lay_out_rows(0)
         lay_out_rows(1)
         transpose_rows(0)
         transpose_rows(1)
+        regroup_weights(1)
+        quantise_weights(0)
         for u in range(UNITS):
             copy_patches(u)
             if u % PAIR == 1 and u // PAIR + 2 < OH:
                 lay_out_rows(u // PAIR + 2)
                 transpose_rows(u // PAIR + 2)
-            if u >= 3 and u + 2 in SCALAR_REGROUPS:
+            if u + 2 < UNITS:
                 regroup_weights(u + 2)
-            if u not in SCALAR_REGROUPS:
-                regroup_weights(u)
-            if u > 0:
-                quantise_patches(u - 1)
-            quantise_weights(u)
-            if u > 0:
-                multiply(u - 1)
+            if u + 1 < UNITS:
+                quantise_weights(u + 1)
+            quantise_patches(u)
+            multiply(u)
             if u >= 3 and u % PAIR == 1:
                 copy_result(u // PAIR - 1)
-        quantise_patches(UNITS - 1)
-        multiply(UNITS - 1)
         copy_result(OH - 1)
 
         nc.sync.dma_start(

@@ -88,7 +88,7 @@ def tile_stdpconvinhibit_s_kernel(tc, in_spikes, weights, out):
             keep.tile([P, UNIT_SLOTS, CO, KW], BF16, name="w_grouped%d" % u, align_bytes=64) for u in range(UNITS)
         ]
         p_grouped = [
-            keep.tile([P, PASSES, PAIR, B, KW], BF16, name="p_grouped%d" % u, align_bytes=64) for u in range(UNITS)
+            keep.tile([P, PAIR, PASSES, B, KW], BF16, name="p_grouped%d" % u, align_bytes=64) for u in range(UNITS)
         ]
 
         def unit_columns(u):
@@ -114,7 +114,7 @@ def tile_stdpconvinhibit_s_kernel(tc, in_spikes, weights, out):
             for e in range(PAIR):
                 j = j0 + e
                 nc.scalar.copy(
-                    out=p_grouped[u][:, :, e].bitcast(F32),
+                    out=p_grouped[u][:, e].bitcast(F32),
                     in_=x_t[(i, j % 2)][:, j // 2 : j // 2 + 2, :].rearrange("p w (b h) -> p h b w", h=PASSES),
                 )
 
@@ -122,15 +122,24 @@ def tile_stdpconvinhibit_s_kernel(tc, in_spikes, weights, out):
             nc.vector.quantize_mx(
                 out=p_codes[:, unit_columns(u)].bitcast(FP8X4),
                 scales=p_scales[:, unit_columns(u)],
-                in_=p_grouped[u][:].rearrange("p h e b v -> p (h e b v)"),
+                in_=p_grouped[u][:].rearrange("p e h b v -> p (e h b v)"),
             )
 
-        def multiply(u):
+        def quantise_patches_of_one(u, e):
+            first = (1 + u * UNIT_SLOTS + e * PASSES) * SLOT
+            columns = slice(first, first + PASSES * SLOT)
+            nc.vector.quantize_mx(
+                out=p_codes[:, columns].bitcast(FP8X4),
+                scales=p_scales[:, columns],
+                in_=p_grouped[u][:, e].rearrange("p h b v -> p (h b v)"),
+            )
+
+        def multiply(u, positions=(0, 1)):
             i, j0 = divmod(u * PAIR, OH)
-            for e in range(PAIR):
+            for e in positions:
                 for h in range(PASSES):
-                    p_slot = 1 + u * UNIT_SLOTS + h * PAIR + e
-                    w_slot = 1 + u * UNIT_SLOTS + e * PASSES + h
+                    p_slot = 1 + u * UNIT_SLOTS + e * PASSES + h
+                    w_slot = p_slot
                     p_win = slice((p_slot - 1) * SLOT, (p_slot + 1) * SLOT)
                     w_win = slice((w_slot - 1) * SLOT, (w_slot + 1) * SLOT)
                     nc.tensor.matmul_mx(
@@ -167,13 +176,17 @@ def tile_stdpconvinhibit_s_kernel(tc, in_spikes, weights, out):
                 regroup_weights(u + 2)
             if u + 1 < UNITS:
                 quantise_weights(u + 1)
-            quantise_patches(u)
-            multiply(u)
-            if u >= 3 and u % PAIR == 1:
-                copy_result(u // PAIR - 1)
-        copy_result(OH - 1)
+            if u + 1 < UNITS:
+                quantise_patches(u)
+                multiply(u)
+            else:
+                for e in range(PAIR):
+                    quantise_patches_of_one(u, e)
+                    multiply(u, (e,))
+        for i in range(OH):
+            copy_result(i)
 
-        nc.sync.dma_start(
+        nc.scalar.dma_start(
             out=out.rearrange("b k i j -> b (k i j)"),
             in_=result[B:P].rearrange("p k q -> p (k q)"),
         )

@@ -154,10 +154,10 @@ def tile_stdpconvinhibit_s_kernel(tc, in_spikes, weights, out):
 
         result = keep.tile([P, CO, OH * OH], F32, name="result")
 
-        def copy_result(i):
+        def copy_result(i, k0=0, k1=CO):
             nc.scalar.copy(
-                out=result[B:P, :, i * OH : (i + 1) * OH],
-                in_=acc[i][B:P, :, SLOT : 2 * SLOT].rearrange("p j k -> p k j"),
+                out=result[B:P, k0:k1, i * OH : (i + 1) * OH],
+                in_=acc[i][B:P, :, SLOT + k0 : SLOT + k1].rearrange("p j k -> p k j"),
             )
 
         regroup_weights(0)
@@ -183,10 +183,13 @@ def tile_stdpconvinhibit_s_kernel(tc, in_spikes, weights, out):
                 for e in range(PAIR):
                     quantise_patches_of_one(u, e)
                     multiply(u, (e,))
-        for i in range(OH):
+        for i in range(OH - 1):
             copy_result(i)
-
-        nc.scalar.dma_start(
-            out=out.rearrange("b k i j -> b (k i j)"),
-            in_=result[B:P].rearrange("p k q -> p (k q)"),
-        )
+        out_rows = out.rearrange("b k i j -> b (k i j)")
+        for half, queue in enumerate((nc.sync, nc.scalar)):
+            k0, k1 = half * CO // 2, (half + 1) * CO // 2
+            copy_result(OH - 1, k0, k1)
+            queue.dma_start(
+                out=out_rows[:, k0 * OH * OH : k1 * OH * OH],
+                in_=result[B:P, k0:k1].rearrange("p k q -> p (k q)"),
+            )

@@ -165,8 +165,8 @@ def tile_stdpconvinhibit_s_kernel(tc, in_spikes, weights, out):
         lay_out_rows(1)
         transpose_rows(0)
         transpose_rows(1)
-        regroup_weights(1)
         quantise_weights(0)
+        regroup_weights(1)
         for u in range(UNITS):
             copy_patches(u)
             if u % PAIR == 1 and u // PAIR + 2 < OH:
@@ -174,11 +174,14 @@ def tile_stdpconvinhibit_s_kernel(tc, in_spikes, weights, out):
                 transpose_rows(u // PAIR + 2)
             if u + 2 < UNITS:
                 regroup_weights(u + 2)
-            if u + 1 < UNITS:
+            if u + 2 < UNITS:
                 quantise_weights(u + 1)
-            if u + 1 < UNITS:
                 quantise_patches(u)
                 multiply(u)
+            elif u + 2 == UNITS:
+                quantise_patches(u)
+                multiply(u)
+                quantise_weights(u + 1)
             else:
                 for e in range(PAIR):
                     quantise_patches_of_one(u, e)

@@ -95,8 +95,8 @@ def tile_stdpconvinhibit_s_kernel(tc, in_spikes, weights, out):
             return slice((1 + u * UNIT_SLOTS) * SLOT, (1 + (u + 1) * UNIT_SLOTS) * SLOT)
 
         def regroup_weights(u):
-            dst = w_grouped[u][:].rearrange("p g (c e) v -> p g c v e", e=4)
-            src = w_raw[u][:].rearrange("p g v (c e) -> p g c v e", e=4)
+            dst = w_grouped[u][:].rearrange("p g (c e) v -> p g c v e", e=8)
+            src = w_raw[u][:].rearrange("p g v (c e) -> p g c v e", e=8)
             if u in SCALAR_REGROUPS:
                 nc.scalar.copy(out=dst, in_=src)
             else:

@@ -23,8 +23,13 @@ UNITS = OH * OH // PAIR
 UNIT_SLOTS = PAIR * PASSES
 RUN = 6
 WORDS = RUN // 2
-SCALAR_REGROUPS = ()
+LEAD = 1
+SPLIT_UNITS = 3
 FLOPS = 2 * OH * OH * B * CI * KW * KW * CO
+
+
+def parts(u):
+    return PAIR if u < SPLIT_UNITS else 1
 
 
 def tile_stdpconvinhibit_s_kernel(tc, in_spikes, weights, out):
@@ -35,14 +40,16 @@ def tile_stdpconvinhibit_s_kernel(tc, in_spikes, weights, out):
         x_sb = keep.tile([P, CL * IH * IH], BF16, name="x_sb")
         w_raw = []
         for u in range(UNITS):
-            if u == 1:
+            if u == 0:
                 nc.sync.dma_start(out=x_sb[:], in_=in_spikes.rearrange("b (h c) r s -> (b h) (c r s)", h=PASSES))
             i, j0 = divmod(u * PAIR, OH)
             raw = keep.tile([P, UNIT_SLOTS, KW, CO], BF16, name="w_raw%d" % u)
-            nc.sync.dma_start(
-                out=raw[:].rearrange("p g v k -> p g (v k)"),
-                in_=weights[i, j0 : j0 + PAIR].rearrange("j (h c) u v k -> (c u) (j h) (v k)", h=PASSES),
-            )
+            n = PAIR // parts(u)
+            for e in range(0, PAIR, n):
+                nc.sync.dma_start(
+                    out=raw[:, e * PASSES : (e + n) * PASSES].rearrange("p g v k -> p g (v k)"),
+                    in_=weights[i, j0 + e : j0 + e + n].rearrange("j (h c) u v k -> (c u) (j h) (v k)", h=PASSES),
+                )
             w_raw.append(raw)
 
         ident = keep.tile([P, P], F32, name="ident")
@@ -97,10 +104,9 @@ def tile_stdpconvinhibit_s_kernel(tc, in_spikes, weights, out):
         def regroup_weights(u):
             dst = w_grouped[u][:].rearrange("p g (c e) v -> p g c v e", e=8)
             src = w_raw[u][:].rearrange("p g v (c e) -> p g c v e", e=8)
-            if u in SCALAR_REGROUPS:
-                nc.scalar.copy(out=dst, in_=src)
-            else:
-                nc.vector.tensor_copy(out=dst, in_=src)
+            n = UNIT_SLOTS // parts(u)
+            for g in range(0, UNIT_SLOTS, n):
+                nc.vector.tensor_copy(out=dst[:, g : g + n], in_=src[:, g : g + n])
 
         def quantise_weights(u):
             nc.vector.quantize_mx(
@@ -160,28 +166,34 @@ def tile_stdpconvinhibit_s_kernel(tc, in_spikes, weights, out):
                 in_=acc[i][B:P, :, SLOT + k0 : SLOT + k1].rearrange("p j k -> p k j"),
             )
 
-        regroup_weights(0)
         lay_out_rows(0)
         lay_out_rows(1)
         transpose_rows(0)
         transpose_rows(1)
-        quantise_weights(0)
-        regroup_weights(1)
-        for u in range(UNITS):
+
+        def prepare_patches(u):
             copy_patches(u)
             if u % PAIR == 1 and u // PAIR + 2 < OH:
                 lay_out_rows(u // PAIR + 2)
                 transpose_rows(u // PAIR + 2)
+
+        regroup_weights(0)
+        quantise_weights(0)
+        regroup_weights(1)
+        for step in range(UNITS + LEAD):
+            if step < UNITS:
+                prepare_patches(step)
+            u = step - LEAD
+            if u < 0:
+                continue
             if u + 2 < UNITS:
                 regroup_weights(u + 2)
-            if u + 2 < UNITS:
                 quantise_weights(u + 1)
+            if u + 1 < UNITS:
                 quantise_patches(u)
                 multiply(u)
-            elif u + 2 == UNITS:
-                quantise_patches(u)
-                multiply(u)
-                quantise_weights(u + 1)
+                if u + 2 == UNITS:
+                    quantise_weights(u + 1)
             else:
                 for e in range(PAIR):
                     quantise_patches_of_one(u, e)

@@ -23,7 +23,8 @@ UNITS = OH * OH // PAIR
 UNIT_SLOTS = PAIR * PASSES
 RUN = 6
 WORDS = RUN // 2
-LEAD = 1
+LEAD = 2
+SCALAR_REGROUPS = {(7, 1): 6}
 SPLIT_UNITS = 3
 FLOPS = 2 * OH * OH * B * CI * KW * KW * CO
 
@@ -101,12 +102,20 @@ def tile_stdpconvinhibit_s_kernel(tc, in_spikes, weights, out):
         def unit_columns(u):
             return slice((1 + u * UNIT_SLOTS) * SLOT, (1 + (u + 1) * UNIT_SLOTS) * SLOT)
 
+        def regroup_position(u, e, copy, n=1):
+            g = slice(e * PASSES, (e + n) * PASSES)
+            copy(
+                out=w_grouped[u][:, g].rearrange("p g (c e) v -> p g c v e", e=8),
+                in_=w_raw[u][:, g].rearrange("p g v (c e) -> p g c v e", e=8),
+            )
+
         def regroup_weights(u):
-            dst = w_grouped[u][:].rearrange("p g (c e) v -> p g c v e", e=8)
-            src = w_raw[u][:].rearrange("p g v (c e) -> p g c v e", e=8)
-            n = UNIT_SLOTS // parts(u)
-            for g in range(0, UNIT_SLOTS, n):
-                nc.vector.tensor_copy(out=dst[:, g : g + n], in_=src[:, g : g + n])
+            mine = [e for e in range(PAIR) if (u, e) not in SCALAR_REGROUPS]
+            if parts(u) == 1 and len(mine) == PAIR:
+                regroup_position(u, 0, nc.vector.tensor_copy, PAIR)
+            else:
+                for e in mine:
+                    regroup_position(u, e, nc.vector.tensor_copy)
 
         def quantise_weights(u):
             nc.vector.quantize_mx(
@@ -178,11 +187,15 @@ def tile_stdpconvinhibit_s_kernel(tc, in_spikes, weights, out):
                 transpose_rows(u // PAIR + 2)
 
         regroup_weights(0)
+        regroup_position(1, 0, nc.vector.tensor_copy)
         quantise_weights(0)
-        regroup_weights(1)
+        regroup_position(1, 1, nc.vector.tensor_copy)
         for step in range(UNITS + LEAD):
             if step < UNITS:
                 prepare_patches(step)
+            for (w, e), at in SCALAR_REGROUPS.items():
+                if at == step:
+                    regroup_position(w, e, nc.scalar.copy)
             u = step - LEAD
             if u < 0:
                 continue

@@ -24,7 +24,8 @@ UNIT_SLOTS = PAIR * PASSES
 RUN = 6
 WORDS = RUN // 2
 LEAD = 2
-SCALAR_REGROUPS = {(7, 1): 6}
+SCALAR_REGROUPS = {(7, 0): 6, (7, 1): 6}
+X_PARTS = 2
 SPLIT_UNITS = 3
 FLOPS = 2 * OH * OH * B * CI * KW * KW * CO
 
@@ -42,7 +43,10 @@ def tile_stdpconvinhibit_s_kernel(tc, in_spikes, weights, out):
         w_raw = []
         for u in range(UNITS):
             if u == 0:
-                nc.sync.dma_start(out=x_sb[:], in_=in_spikes.rearrange("b (h c) r s -> (b h) (c r s)", h=PASSES))
+                x_in = in_spikes.rearrange("b (h c) r s -> (b h) (c r s)", h=PASSES)
+                for part in range(X_PARTS):
+                    run = slice(part * CL // X_PARTS * IH * IH, (part + 1) * CL // X_PARTS * IH * IH)
+                    nc.sync.dma_start(out=x_sb[:, run], in_=x_in[:, run])
             i, j0 = divmod(u * PAIR, OH)
             raw = keep.tile([P, UNIT_SLOTS, KW, CO], BF16, name="w_raw%d" % u)
             n = PAIR // parts(u)
@@ -70,13 +74,13 @@ def tile_stdpconvinhibit_s_kernel(tc, in_spikes, weights, out):
         x_runs = [keep.tile([P, 2, CL, KW, RUN], BF16, name="x_runs%d" % i) for i in range(OH)]
         x_t = {}
 
-        def lay_out_rows(i):
-            for parity in range(2):
-                src = x_img[:, :, i : i + KW, parity : parity + RUN]
-                if i == 0:
-                    nc.vector.tensor_copy(out=x_runs[i][:, parity], in_=src)
-                else:
-                    nc.scalar.copy(out=x_runs[i][:, parity], in_=src)
+        def lay_out_rows(i, parity, copy, n=1):
+            for c in range(0, CL, CL // n):
+                rows = slice(c, c + CL // n)
+                copy(
+                    out=x_runs[i][:, parity, rows],
+                    in_=x_img[:, rows, i : i + KW, parity : parity + RUN],
+                )
 
         def transpose_rows(i):
             for parity in range(2):
@@ -124,14 +128,13 @@ def tile_stdpconvinhibit_s_kernel(tc, in_spikes, weights, out):
                 in_=w_grouped[u][:].rearrange("p g k v -> p (g k v)"),
             )
 
-        def copy_patches(u):
+        def copy_patches(u, e):
             i, j0 = divmod(u * PAIR, OH)
-            for e in range(PAIR):
-                j = j0 + e
-                nc.scalar.copy(
-                    out=p_grouped[u][:, e].bitcast(F32),
-                    in_=x_t[(i, j % 2)][:, j // 2 : j // 2 + 2, :].rearrange("p w (b h) -> p h b w", h=PASSES),
-                )
+            j = j0 + e
+            nc.scalar.copy(
+                out=p_grouped[u][:, e].bitcast(F32),
+                in_=x_t[(i, j % 2)][:, j // 2 : j // 2 + 2, :].rearrange("p w (b h) -> p h b w", h=PASSES),
+            )
 
         def quantise_patches(u):
             nc.vector.quantize_mx(
@@ -175,16 +178,25 @@ def tile_stdpconvinhibit_s_kernel(tc, in_spikes, weights, out):
                 in_=acc[i][B:P, :, SLOT + k0 : SLOT + k1].rearrange("p j k -> p k j"),
             )
 
-        lay_out_rows(0)
-        lay_out_rows(1)
+        for n in range(X_PARTS):
+            c = slice(n * CL // X_PARTS, (n + 1) * CL // X_PARTS)
+            for i, copy in ((0, nc.vector.tensor_copy), (1, nc.scalar.copy)):
+                for parity in range(2):
+                    copy(out=x_runs[i][:, parity, c], in_=x_img[:, c, i : i + KW, parity : parity + RUN])
         transpose_rows(0)
         transpose_rows(1)
 
         def prepare_patches(u):
-            copy_patches(u)
-            if u % PAIR == 1 and u // PAIR + 2 < OH:
-                lay_out_rows(u // PAIR + 2)
-                transpose_rows(u // PAIR + 2)
+            for e in range(PAIR):
+                if u == 0:
+                    lay_out_rows(2, e, nc.scalar.copy)
+                copy_patches(u, e)
+            i = u // PAIR + 2
+            if u % PAIR == 1 and i < OH:
+                for parity in range(2):
+                    if i > 2:
+                        lay_out_rows(i, parity, nc.scalar.copy)
+                transpose_rows(i)
 
         regroup_weights(0)
         regroup_position(1, 0, nc.vector.tensor_copy)
@@ -201,12 +213,10 @@ def tile_stdpconvinhibit_s_kernel(tc, in_spikes, weights, out):
                 continue
             if u + 2 < UNITS:
                 regroup_weights(u + 2)
-                quantise_weights(u + 1)
             if u + 1 < UNITS:
                 quantise_patches(u)
                 multiply(u)
-                if u + 2 == UNITS:
-                    quantise_weights(u + 1)
+                quantise_weights(u + 1)
             else:
                 for e in range(PAIR):
                     quantise_patches_of_one(u, e)

@@ -18,6 +18,7 @@ KW = 4
 PASSES = 2
 CL = CI // PASSES
 SLOT = 64
+LATE = SLOT // 2
 PAIR = 2
 UNITS = OH * OH // PAIR
 UNIT_SLOTS = PAIR * PASSES
@@ -25,6 +26,7 @@ RUN = 6
 WORDS = RUN // 2
 LEAD = 2
 SCALAR_REGROUPS = {(7, 0): 6, (7, 1): 6}
+PAIRED = (1, 2)
 X_PARTS = 2
 SPLIT_UNITS = 3
 FLOPS = 2 * OH * OH * B * CI * KW * KW * CO
@@ -61,14 +63,14 @@ def tile_stdpconvinhibit_s_kernel(tc, in_spikes, weights, out):
         make_identity(nc, ident[:])
 
         n_slots = 1 + UNITS * UNIT_SLOTS
+        p_grouped = keep.tile([P, n_slots * SLOT, KW], BF16, name="p_grouped", align_bytes=64)
         p_codes = keep.tile([P, n_slots * SLOT], U32, name="p_codes", align_bytes=64)
         p_scales = keep.tile([P, n_slots * SLOT], U8, name="p_scales", align_bytes=64)
         w_codes = keep.tile([P, n_slots * SLOT], U32, name="w_codes", align_bytes=64)
         w_scales = keep.tile([P, n_slots * SLOT], U8, name="w_scales", align_bytes=64)
-        for codes in (p_codes, w_codes):
-            nc.vector.memset(codes[:, 0:SLOT].bitcast(I32), 0)
-        for scales in (p_scales, w_scales):
-            nc.vector.memset(scales[:, 0:SLOT].bitcast(I32), 0)
+        nc.vector.memset(p_grouped[:, 0:LATE, :], 0.0)
+        for tile, spare in ((p_codes, n_slots - 1), (p_scales, n_slots - 1), (w_codes, 0), (w_scales, 0)):
+            nc.vector.memset(tile[:, spare * SLOT : (spare + 1) * SLOT].bitcast(I32), 0)
 
         x_img = x_sb[:].rearrange("p (c r s) -> p c r s", c=CL, r=IH, s=IH)
         x_runs = [keep.tile([P, 2, CL, KW, RUN], BF16, name="x_runs%d" % i) for i in range(OH)]
@@ -96,12 +98,10 @@ def tile_stdpconvinhibit_s_kernel(tc, in_spikes, weights, out):
                 x_t[(i, parity)] = bank
 
         acc = [psum.tile([P, OH, 2 * SLOT], F32, name="acc%d" % i) for i in range(OH)]
-        w_grouped = [
-            keep.tile([P, UNIT_SLOTS, CO, KW], BF16, name="w_grouped%d" % u, align_bytes=64) for u in range(UNITS)
+        w_pairs = [
+            keep.tile([P, 2 * UNIT_SLOTS, CO, KW], BF16, name="w_grouped%d" % v, align_bytes=64) for v in range(UNITS // 2)
         ]
-        p_grouped = [
-            keep.tile([P, PAIR, PASSES, B, KW], BF16, name="p_grouped%d" % u, align_bytes=64) for u in range(UNITS)
-        ]
+        w_grouped = [w_pairs[u // 2][:, u % 2 * UNIT_SLOTS : (u % 2 + 1) * UNIT_SLOTS] for u in range(UNITS)]
 
         def unit_columns(u):
             return slice((1 + u * UNIT_SLOTS) * SLOT, (1 + (u + 1) * UNIT_SLOTS) * SLOT)
@@ -125,63 +125,62 @@ def tile_stdpconvinhibit_s_kernel(tc, in_spikes, weights, out):
             nc.vector.quantize_mx(
                 out=w_codes[:, unit_columns(u)].bitcast(FP8X4),
                 scales=w_scales[:, unit_columns(u)],
-                in_=w_grouped[u][:].rearrange("p g k v -> p (g k v)"),
+                in_=w_grouped[u].rearrange("p g k v -> p (g k v)"),
+            )
+
+        def quantise_pair(v):
+            win = slice(unit_columns(2 * v).start, unit_columns(2 * v + 1).stop)
+            nc.vector.quantize_mx(
+                out=w_codes[:, win].bitcast(FP8X4),
+                scales=w_scales[:, win],
+                in_=w_pairs[v][:].rearrange("p g k v -> p (g k v)"),
             )
 
         def copy_patches(u, e):
             i, j0 = divmod(u * PAIR, OH)
             j = j0 + e
+            first = (u * PAIR + e) * PASSES * SLOT + LATE
+            patches = p_grouped[:, first : first + PASSES * SLOT, :].rearrange("p n v -> p (n v)").bitcast(F32)
             nc.scalar.copy(
-                out=p_grouped[u][:, e].bitcast(F32),
+                out=patches.rearrange("p (h b w) -> p h b w", h=PASSES, b=B),
                 in_=x_t[(i, j % 2)][:, j // 2 : j // 2 + 2, :].rearrange("p w (b h) -> p h b w", h=PASSES),
             )
 
-        def quantise_patches(u):
+        def quantise_patches(first, n):
+            win = slice(first, first + n)
             nc.vector.quantize_mx(
-                out=p_codes[:, unit_columns(u)].bitcast(FP8X4),
-                scales=p_scales[:, unit_columns(u)],
-                in_=p_grouped[u][:].rearrange("p e h b v -> p (e h b v)"),
+                out=p_codes[:, win].bitcast(FP8X4),
+                scales=p_scales[:, win],
+                in_=p_grouped[:, win, :].rearrange("p n v -> p (n v)"),
             )
 
-        def quantise_patches_of_one(u, e):
-            first = (1 + u * UNIT_SLOTS + e * PASSES) * SLOT
-            columns = slice(first, first + PASSES * SLOT)
-            nc.vector.quantize_mx(
-                out=p_codes[:, columns].bitcast(FP8X4),
-                scales=p_scales[:, columns],
-                in_=p_grouped[u][:, e].rearrange("p h b v -> p (h b v)"),
-            )
-
-        def multiply(u, positions=(0, 1)):
+        def multiply(u, e, h):
             i, j0 = divmod(u * PAIR, OH)
-            for e in positions:
-                for h in range(PASSES):
-                    p_slot = 1 + u * UNIT_SLOTS + e * PASSES + h
-                    w_slot = p_slot
-                    p_win = slice((p_slot - 1) * SLOT, (p_slot + 1) * SLOT)
-                    w_win = slice((w_slot - 1) * SLOT, (w_slot + 1) * SLOT)
-                    nc.tensor.matmul_mx(
-                        out=acc[i][:, j0 + e, :],
-                        lhsT=p_codes[:, p_win].bitcast(FP8X4),
-                        lhsT_scale=p_scales[:, p_win],
-                        rhs=w_codes[:, w_win].bitcast(FP8X4),
-                        rhs_scale=w_scales[:, w_win],
-                        start=(h == 0),
-                        stop=(h == PASSES - 1),
-                    )
+            slot = u * UNIT_SLOTS + e * PASSES + h
+            win = slice(slot * SLOT, (slot + 2) * SLOT)
+            nc.tensor.matmul_mx(
+                out=acc[i][:, j0 + e, :],
+                lhsT=p_codes[:, win].bitcast(FP8X4),
+                lhsT_scale=p_scales[:, win],
+                rhs=w_codes[:, win].bitcast(FP8X4),
+                rhs_scale=w_scales[:, win],
+                start=(h == 0),
+                stop=(h == PASSES - 1),
+            )
 
         result = keep.tile([P, CO, OH * OH], F32, name="result")
 
         def copy_result(i, k0=0, k1=CO):
             nc.scalar.copy(
-                out=result[B:P, k0:k1, i * OH : (i + 1) * OH],
-                in_=acc[i][B:P, :, SLOT + k0 : SLOT + k1].rearrange("p j k -> p k j"),
+                out=result[:, k0:k1, i * OH : (i + 1) * OH],
+                in_=acc[i][:, :, SLOT + k0 : SLOT + k1].rearrange("p j k -> p k j"),
             )
 
         for n in range(X_PARTS):
             c = slice(n * CL // X_PARTS, (n + 1) * CL // X_PARTS)
-            for i, copy in ((0, nc.vector.tensor_copy), (1, nc.scalar.copy)):
+            for i in range(2):
                 for parity in range(2):
+                    copy = nc.vector.tensor_copy if (i == 0 or parity == 1) else nc.scalar.copy
                     copy(out=x_runs[i][:, parity, c], in_=x_img[:, c, i : i + KW, parity : parity + RUN])
         transpose_rows(0)
         transpose_rows(1)
@@ -213,14 +212,28 @@ def tile_stdpconvinhibit_s_kernel(tc, in_spikes, weights, out):
                 continue
             if u + 2 < UNITS:
                 regroup_weights(u + 2)
+            if u % 2 == 0 and u // 2 in PAIRED:
+                quantise_pair(u // 2)
+            first = u * UNIT_SLOTS * SLOT
             if u + 1 < UNITS:
-                quantise_patches(u)
-                multiply(u)
-                quantise_weights(u + 1)
+                quantise_patches(first, UNIT_SLOTS * SLOT)
+                if u > 0:
+                    for h in range(PASSES):
+                        multiply(u - 1, 1, h)
+                for h in range(PASSES):
+                    multiply(u, 0, h)
+                if (u + 1) // 2 not in PAIRED:
+                    quantise_weights(u + 1)
             else:
-                for e in range(PAIR):
-                    quantise_patches_of_one(u, e)
-                    multiply(u, (e,))
+                quantise_patches(first, 2 * SLOT)
+                for h in range(PASSES):
+                    multiply(u - 1, 1, h)
+                multiply(u, 0, 0)
+                quantise_patches(first + 2 * SLOT, 2 * SLOT)
+                multiply(u, 0, 1)
+                multiply(u, 1, 0)
+                quantise_patches(first + 4 * SLOT, LATE)
+                multiply(u, 1, 1)
         for i in range(OH - 1):
             copy_result(i)
         out_rows = out.rearrange("b k i j -> b (k i j)")
@@ -229,5 +242,5 @@ def tile_stdpconvinhibit_s_kernel(tc, in_spikes, weights, out):
             copy_result(OH - 1, k0, k1)
             queue.dma_start(
                 out=out_rows[:, k0 * OH * OH : k1 * OH * OH],
-                in_=result[B:P, k0:k1].rearrange("p k q -> p (k q)"),
+                in_=result[LATE : LATE + B, k0:k1].rearrange("p k q -> p (k q)"),
             )

@@ -201,6 +201,9 @@ def tile_stdpconvinhibit_s_kernel(tc, in_spikes, weights, out):
         regroup_position(1, 0, nc.vector.tensor_copy)
         quantise_weights(0)
         regroup_position(1, 1, nc.vector.tensor_copy)
+        regroup_position(2, 0, nc.vector.tensor_copy)
+        quantise_weights(1)
+        regroup_position(2, 1, nc.vector.tensor_copy)
         for step in range(UNITS + LEAD):
             if step < UNITS:
                 prepare_patches(step)
@@ -210,24 +213,24 @@ def tile_stdpconvinhibit_s_kernel(tc, in_spikes, weights, out):
             u = step - LEAD
             if u < 0:
                 continue
-            if u + 2 < UNITS:
+            if 0 < u < UNITS - 2:
                 regroup_weights(u + 2)
             if u % 2 == 0 and u // 2 in PAIRED:
                 quantise_pair(u // 2)
             first = u * UNIT_SLOTS * SLOT
             if u + 1 < UNITS:
-                quantise_patches(first, UNIT_SLOTS * SLOT)
+                if u != 3:
+                    quantise_patches(first, UNIT_SLOTS * SLOT * (2 if u == 2 else 1))
                 if u > 0:
-                    for h in range(PASSES):
-                        multiply(u - 1, 1, h)
-                for h in range(PASSES):
-                    multiply(u, 0, h)
-                if (u + 1) // 2 not in PAIRED:
+                    multiply(u - 1, 1, 1)
+                multiply(u, 0, 0)
+                multiply(u, 0, 1)
+                multiply(u, 1, 0)
+                if u > 0 and (u + 1) // 2 not in PAIRED:
                     quantise_weights(u + 1)
             else:
                 quantise_patches(first, 2 * SLOT)
-                for h in range(PASSES):
-                    multiply(u - 1, 1, h)
+                multiply(u - 1, 1, 1)
                 multiply(u, 0, 0)
                 quantise_patches(first + 2 * SLOT, 2 * SLOT)
                 multiply(u, 0, 1)
@@ -237,10 +240,11 @@ def tile_stdpconvinhibit_s_kernel(tc, in_spikes, weights, out):
         for i in range(OH - 1):
             copy_result(i)
         out_rows = out.rearrange("b k i j -> b (k i j)")
-        for half, queue in enumerate((nc.sync, nc.scalar)):
-            k0, k1 = half * CO // 2, (half + 1) * CO // 2
-            copy_result(OH - 1, k0, k1)
+        k0 = 0
+        for n, queue in zip((16, 24, 24), (nc.sync, nc.sync, nc.scalar)):
+            copy_result(OH - 1, k0, k0 + n)
             queue.dma_start(
-                out=out_rows[:, k0 * OH * OH : k1 * OH * OH],
-                in_=result[LATE : LATE + B, k0:k1].rearrange("p k q -> p (k q)"),
+                out=out_rows[:, k0 * OH * OH : (k0 + n) * OH * OH],
+                in_=result[LATE : LATE + B, k0 : k0 + n].rearrange("p k q -> p (k q)"),
             )
+            k0 += n

@@ -240,11 +240,10 @@ def tile_stdpconvinhibit_s_kernel(tc, in_spikes, weights, out):
         for i in range(OH - 1):
             copy_result(i)
         out_rows = out.rearrange("b k i j -> b (k i j)")
-        k0 = 0
-        for n, queue in zip((16, 24, 24), (nc.sync, nc.sync, nc.scalar)):
-            copy_result(OH - 1, k0, k0 + n)
+        for half, queue in enumerate((nc.sync, nc.scalar)):
+            k0, k1 = half * CO // 2, (half + 1) * CO // 2
+            copy_result(OH - 1, k0, k1)
             queue.dma_start(
-                out=out_rows[:, k0 * OH * OH : (k0 + n) * OH * OH],
-                in_=result[LATE : LATE + B, k0 : k0 + n].rearrange("p k q -> p (k q)"),
+                out=out_rows[:, k0 * OH * OH : k1 * OH * OH],
+                in_=result[LATE : LATE + B, k0:k1].rearrange("p k q -> p (k q)"),
             )
-            k0 += n

import concourse.mybir as mybir
from concourse.masks import make_identity

BF16 = mybir.dt.bfloat16
F32 = mybir.dt.float32
I32 = mybir.dt.int32
U32 = mybir.dt.uint32
U8 = mybir.dt.uint8
FP8X4 = mybir.dt.float8_e4m3fn_x4

P = 128
B = 64
CI = 64
CO = 64
IH = 7
OH = 4
KW = 4
PASSES = 2
CL = CI // PASSES
SLOT = 64
LATE = SLOT // 2
PAIR = 2
UNITS = OH * OH // PAIR
UNIT_SLOTS = PAIR * PASSES
RUN = 6
WORDS = RUN // 2
LEAD = 2
SCALAR_REGROUPS = {(7, 0): 6, (7, 1): 6}
PAIRED = (1, 2)
X_PARTS = 2
SPLIT_UNITS = 3
FLOPS = 2 * OH * OH * B * CI * KW * KW * CO


def parts(u):
    return PAIR if u < SPLIT_UNITS else 1


def tile_stdpconvinhibit_s_kernel(tc, in_spikes, weights, out):
    nc = tc.nc
    with tc.tile_pool(name="keep", bufs=1) as keep, tc.psum_pool(name="psum", bufs=1) as psum, tc.psum_pool(
        name="turned", bufs=4
    ) as turned, tc.manual_schedule():
        x_sb = keep.tile([P, CL * IH * IH], BF16, name="x_sb")
        w_raw = []
        for u in range(UNITS):
            if u == 0:
                x_in = in_spikes.rearrange("b (h c) r s -> (b h) (c r s)", h=PASSES)
                for part in range(X_PARTS):
                    run = slice(part * CL // X_PARTS * IH * IH, (part + 1) * CL // X_PARTS * IH * IH)
                    nc.sync.dma_start(out=x_sb[:, run], in_=x_in[:, run])
            i, j0 = divmod(u * PAIR, OH)
            raw = keep.tile([P, UNIT_SLOTS, KW, CO], BF16, name="w_raw%d" % u)
            n = PAIR // parts(u)
            for e in range(0, PAIR, n):
                nc.sync.dma_start(
                    out=raw[:, e * PASSES : (e + n) * PASSES].rearrange("p g v k -> p g (v k)"),
                    in_=weights[i, j0 + e : j0 + e + n].rearrange("j (h c) u v k -> (c u) (j h) (v k)", h=PASSES),
                )
            w_raw.append(raw)

        ident = keep.tile([P, P], F32, name="ident")
        make_identity(nc, ident[:])

        n_slots = 1 + UNITS * UNIT_SLOTS
        p_grouped = keep.tile([P, n_slots * SLOT, KW], BF16, name="p_grouped", align_bytes=64)
        p_codes = keep.tile([P, n_slots * SLOT], U32, name="p_codes", align_bytes=64)
        p_scales = keep.tile([P, n_slots * SLOT], U8, name="p_scales", align_bytes=64)
        w_codes = keep.tile([P, n_slots * SLOT], U32, name="w_codes", align_bytes=64)
        w_scales = keep.tile([P, n_slots * SLOT], U8, name="w_scales", align_bytes=64)
        nc.vector.memset(p_grouped[:, 0:LATE, :], 0.0)
        for tile, spare in ((p_codes, n_slots - 1), (p_scales, n_slots - 1), (w_codes, 0), (w_scales, 0)):
            nc.vector.memset(tile[:, spare * SLOT : (spare + 1) * SLOT].bitcast(I32), 0)

        x_img = x_sb[:].rearrange("p (c r s) -> p c r s", c=CL, r=IH, s=IH)
        x_runs = [keep.tile([P, 2, CL, KW, RUN], BF16, name="x_runs%d" % i) for i in range(OH)]
        x_t = {}

        def lay_out_rows(i, parity, copy, n=1):
            for c in range(0, CL, CL // n):
                rows = slice(c, c + CL // n)
                copy(
                    out=x_runs[i][:, parity, rows],
                    in_=x_img[:, rows, i : i + KW, parity : parity + RUN],
                )

        def transpose_rows(i):
            for parity in range(2):
                words = (
                    x_runs[i][:, parity]
                    .rearrange("p c u s -> p (c u s)")
                    .bitcast(F32)
                    .rearrange("p (n w) -> p n w", w=WORDS)
                )
                bank = turned.tile([P, WORDS, P], F32, name="x_t")
                for w in range(WORDS):
                    nc.tensor.transpose(bank[:, w, :], words[:, :, w], ident[:])
                x_t[(i, parity)] = bank

        acc = [psum.tile([P, OH, 2 * SLOT], F32, name="acc%d" % i) for i in range(OH)]
        w_pairs = [
            keep.tile([P, 2 * UNIT_SLOTS, CO, KW], BF16, name="w_grouped%d" % v, align_bytes=64) for v in range(UNITS // 2)
        ]
        w_grouped = [w_pairs[u // 2][:, u % 2 * UNIT_SLOTS : (u % 2 + 1) * UNIT_SLOTS] for u in range(UNITS)]

        def unit_columns(u):
            return slice((1 + u * UNIT_SLOTS) * SLOT, (1 + (u + 1) * UNIT_SLOTS) * SLOT)

        def regroup_position(u, e, copy, n=1):
            g = slice(e * PASSES, (e + n) * PASSES)
            copy(
                out=w_grouped[u][:, g].rearrange("p g (c e) v -> p g c v e", e=8),
                in_=w_raw[u][:, g].rearrange("p g v (c e) -> p g c v e", e=8),
            )

        def regroup_weights(u):
            mine = [e for e in range(PAIR) if (u, e) not in SCALAR_REGROUPS]
            if parts(u) == 1 and len(mine) == PAIR:
                regroup_position(u, 0, nc.vector.tensor_copy, PAIR)
            else:
                for e in mine:
                    regroup_position(u, e, nc.vector.tensor_copy)

        def quantise_weights(u):
            nc.vector.quantize_mx(
                out=w_codes[:, unit_columns(u)].bitcast(FP8X4),
                scales=w_scales[:, unit_columns(u)],
                in_=w_grouped[u].rearrange("p g k v -> p (g k v)"),
            )

        def quantise_pair(v):
            win = slice(unit_columns(2 * v).start, unit_columns(2 * v + 1).stop)
            nc.vector.quantize_mx(
                out=w_codes[:, win].bitcast(FP8X4),
                scales=w_scales[:, win],
                in_=w_pairs[v][:].rearrange("p g k v -> p (g k v)"),
            )

        def copy_patches(u, e):
            i, j0 = divmod(u * PAIR, OH)
            j = j0 + e
            first = (u * PAIR + e) * PASSES * SLOT + LATE
            patches = p_grouped[:, first : first + PASSES * SLOT, :].rearrange("p n v -> p (n v)").bitcast(F32)
            nc.scalar.copy(
                out=patches.rearrange("p (h b w) -> p h b w", h=PASSES, b=B),
                in_=x_t[(i, j % 2)][:, j // 2 : j // 2 + 2, :].rearrange("p w (b h) -> p h b w", h=PASSES),
            )

        def quantise_patches(first, n):
            win = slice(first, first + n)
            nc.vector.quantize_mx(
                out=p_codes[:, win].bitcast(FP8X4),
                scales=p_scales[:, win],
                in_=p_grouped[:, win, :].rearrange("p n v -> p (n v)"),
            )

        def multiply(u, e, h):
            i, j0 = divmod(u * PAIR, OH)
            slot = u * UNIT_SLOTS + e * PASSES + h
            win = slice(slot * SLOT, (slot + 2) * SLOT)
            nc.tensor.matmul_mx(
                out=acc[i][:, j0 + e, :],
                lhsT=p_codes[:, win].bitcast(FP8X4),
                lhsT_scale=p_scales[:, win],
                rhs=w_codes[:, win].bitcast(FP8X4),
                rhs_scale=w_scales[:, win],
                start=(h == 0),
                stop=(h == PASSES - 1),
            )

        result = keep.tile([P, CO, OH * OH], F32, name="result")

        def copy_result(i, k0=0, k1=CO):
            nc.scalar.copy(
                out=result[:, k0:k1, i * OH : (i + 1) * OH],
                in_=acc[i][:, :, SLOT + k0 : SLOT + k1].rearrange("p j k -> p k j"),
            )

        for n in range(X_PARTS):
            c = slice(n * CL // X_PARTS, (n + 1) * CL // X_PARTS)
            for i in range(2):
                for parity in range(2):
                    copy = nc.vector.tensor_copy if (i == 0 or parity == 1) else nc.scalar.copy
                    copy(out=x_runs[i][:, parity, c], in_=x_img[:, c, i : i + KW, parity : parity + RUN])
        transpose_rows(0)
        transpose_rows(1)

        def prepare_patches(u):
            for e in range(PAIR):
                if u == 0:
                    lay_out_rows(2, e, nc.scalar.copy)
                copy_patches(u, e)
            i = u // PAIR + 2
            if u % PAIR == 1 and i < OH:
                for parity in range(2):
                    if i > 2:
                        lay_out_rows(i, parity, nc.scalar.copy)
                transpose_rows(i)

        regroup_weights(0)
        regroup_position(1, 0, nc.vector.tensor_copy)
        quantise_weights(0)
        regroup_position(1, 1, nc.vector.tensor_copy)
        regroup_position(2, 0, nc.vector.tensor_copy)
        quantise_weights(1)
        regroup_position(2, 1, nc.vector.tensor_copy)
        for step in range(UNITS + LEAD):
            if step < UNITS:
                prepare_patches(step)
            for (w, e), at in SCALAR_REGROUPS.items():
                if at == step:
                    regroup_position(w, e, nc.scalar.copy)
            u = step - LEAD
            if u < 0:
                continue
            if 0 < u < UNITS - 2:
                regroup_weights(u + 2)
            if u % 2 == 0 and u // 2 in PAIRED:
                quantise_pair(u // 2)
            first = u * UNIT_SLOTS * SLOT
            if u + 1 < UNITS:
                if u != 3:
                    quantise_patches(first, UNIT_SLOTS * SLOT * (2 if u == 2 else 1))
                if u > 0:
                    multiply(u - 1, 1, 1)
                multiply(u, 0, 0)
                multiply(u, 0, 1)
                multiply(u, 1, 0)
                if u > 0 and (u + 1) // 2 not in PAIRED:
                    quantise_weights(u + 1)
            else:
                quantise_patches(first, 2 * SLOT)
                multiply(u - 1, 1, 1)
                multiply(u, 0, 0)
                quantise_patches(first + 2 * SLOT, 2 * SLOT)
                multiply(u, 0, 1)
                multiply(u, 1, 0)
                quantise_patches(first + 4 * SLOT, LATE)
                multiply(u, 1, 1)
        for i in range(OH - 1):
            copy_result(i)
        out_rows = out.rearrange("b k i j -> b (k i j)")
        for half, queue in enumerate((nc.sync, nc.scalar)):
            k0, k1 = half * CO // 2, (half + 1) * CO // 2
            copy_result(OH - 1, k0, k1)
            queue.dma_start(
                out=out_rows[:, k0 * OH * OH : k1 * OH * OH],
                in_=result[LATE : LATE + B, k0:k1].rearrange("p k q -> p (k q)"),
            )
